import numpy as np
import ml_dtypes


def mxq(x, axis, fmt="e4m3"):
    dtype, down = {"e4m3": (ml_dtypes.float8_e4m3fn, 7), "e5m2": (ml_dtypes.float8_e5m2, 14)}[fmt]
    v = np.moveaxis(np.asarray(x, np.float32).astype(ml_dtypes.bfloat16).astype(np.float64), axis, -1)
    blocks = v.reshape(v.shape[:-1] + (-1, 32))
    amax = np.abs(blocks).max(-1, keepdims=True)
    byte = np.maximum(np.where(amax > 0, np.frexp(amax)[1] - 1 + 127, 0) - down, 1)
    scale = np.exp2(byte - 127.0)
    codes = (blocks / scale).astype(np.float32).astype(dtype).astype(np.float64)
    return np.moveaxis((codes * scale).reshape(v.shape), -1, axis)


WIDE = False


def mx_kscale(k):
    if not WIDE:
        return np.ones(k)
    levels = np.array([10, -10, 5, -5, 0])
    a = np.random.permutation(np.resize(levels, k // 512 * 4)).reshape(k // 512, 4)
    idx = np.arange(k)
    return np.exp2(a[idx // 512, idx % 128 // 32])


BF16 = ml_dtypes.bfloat16


def bf(x):
    return np.asarray(x, np.float32).astype(BF16)


def f64(x):
    return np.asarray(x).astype(np.float64)


E2M1 = np.array([0.0, 0.5, 1.0, 1.5, 2.0, 3.0, 4.0, 6.0, -0.0, -0.5, -1.0, -1.5, -2.0, -3.0, -4.0, -6.0])


def pack_weight(w, fmt):
    k, n = w.shape
    w = f64(bf(w)).reshape(k // 32, 32, n)
    amax = np.abs(w).max(1)
    if fmt == "e4m3":
        byte = np.frexp(amax)[1] - 1 + 127 - 7
    else:
        mant, ex = np.frexp(amax / 6.0)
        byte = np.where(mant > 0.5, ex, ex - 1) + 127
    byte = np.clip(np.where(amax > 0, byte, 1), 1, 254)
    scaled = (w * np.exp2(127.0 - byte)[:, None, :]).reshape(k, n).astype(np.float32)
    by_word = np.ascontiguousarray(scaled.reshape(k // 512, 128, 4, n).transpose(0, 1, 3, 2))
    if fmt == "e4m3":
        words = by_word.astype(ml_dtypes.float8_e4m3fn).view(np.uint8)
    else:
        c = by_word.astype(ml_dtypes.float4_e2m1fn).view(np.uint8) & 0xF
        words = c[..., 0::2] | (c[..., 1::2] << 4)
    return np.ascontiguousarray(words), np.ascontiguousarray(byte.astype(np.uint8).reshape(k // 512, 16, n))


def unpack_weight(words, scales, fmt):
    g, p, n, _ = words.shape
    if fmt == "e4m3":
        vals = np.ascontiguousarray(words).view(ml_dtypes.float8_e4m3fn).astype(np.float64)
    else:
        nib = np.empty((g, p, n, 4), np.uint8)
        nib[..., 0::2] = words & 0xF
        nib[..., 1::2] = words >> 4
        vals = E2M1[nib]
    vals = vals * np.repeat(np.exp2(scales.astype(np.float64) - 127.0), 8, axis=1)[..., None]
    return vals.transpose(0, 1, 3, 2).reshape(g * 512, n)


N, C_IN, H_IN, W_IN, C_OUT, K, PAD, STRIDE = 128, 64, 9, 9, 128, 4, 1, 1
H_OUT = (H_IN - K + 2 * PAD) // STRIDE + 1
W_OUT = (W_IN - K + 2 * PAD) // STRIDE + 1
RF = C_IN * K * K
NUM_PIX = H_OUT * W_OUT


def _unfold(x):
    n = x.shape[0]
    xp = np.pad(x, ((0, 0), (0, 0), (PAD, PAD), (PAD, PAD)))
    patches = []
    for i in range(K):
        for j in range(K):
            patches.append(xp[:, :, i:i + H_OUT * STRIDE:STRIDE, j:j + W_OUT * STRIDE:STRIDE])
    p = np.stack(patches, axis=2)
    return p.reshape(n, RF, NUM_PIX)


def setup_inputs():
    sc = mx_kscale(RF)[::K * K]
    s = np.repeat(sc, K * K)
    x = bf(np.random.standard_normal((N, C_IN, H_IN, W_IN)) * sc[None, :, None, None])
    stack = np.random.standard_normal((C_OUT, RF, NUM_PIX)) / np.sqrt(RF) / s[None, :, None]
    words, scales = pack_weight(stack.reshape(-1, NUM_PIX), "e4m3")
    bias = bf(np.random.standard_normal((C_OUT, NUM_PIX)) * 0.3)
    return {"x": x, "filters_words": words, "filters_scales": scales, "bias": bias}


def reference(x, filters_words, filters_scales, bias):
    x = f64(x)
    f_hat = _unfold(x)
    fq = mxq(f_hat, 1, "e4m3")
    wq = unpack_weight(filters_words, filters_scales, "e4m3").reshape(C_OUT, RF, NUM_PIX)
    g = (fq.transpose(2, 0, 1) @ wq.transpose(2, 1, 0)).transpose(1, 2, 0)
    g = g + f64(bias)
    return g.reshape(x.shape[0], C_OUT, H_OUT, W_OUT)

@@ -1,0 +1,229 @@
+from contextlib import ExitStack
+
+import concourse.mybir as mybir
+from concourse.masks import make_identity
+
+BF16 = mybir.dt.bfloat16
+F32 = mybir.dt.float32
+I32 = mybir.dt.int32
+U32 = mybir.dt.uint32
+U8 = mybir.dt.uint8
+FP8X4 = mybir.dt.float8_e4m3fn_x4
+
+P = 128
+IMAGES = 128
+C_IN = 64
+SIDE_IN = 9
+SIDE_OUT = 8
+TAPS = 4
+C_OUT = 128
+PIXELS = SIDE_OUT * SIDE_OUT
+PASSES = 2
+CH_PASS = C_IN // PASSES
+ROW = SIDE_IN + 1
+ROW_WORDS = ROW // 2
+PAIR_WORDS = 2 * PASSES * ROW_WORDS
+PAIR_PITCH = 24
+BANK_PLANES = 4
+O_CHUNK = 32
+CHUNKS = C_OUT // O_CHUNK
+PX_GROUP = 4
+GROUPS_ROW = SIDE_OUT // PX_GROUP
+N_MOVING = O_CHUNK * PX_GROUP
+BANK = 512
+LAG = 3
+
+FLOPS = 2 * IMAGES * C_IN * TAPS * TAPS * C_OUT * PIXELS
+
+
+def tile_localconv2dlayer_e_kernel(tc, x, filters_words, filters_scales, bias, out):
+    nc = tc.nc
+    with ExitStack() as stack:
+        keep = stack.enter_context(tc.tile_pool(name="keep", bufs=1))
+        raw_pool = stack.enter_context(tc.tile_pool(name="raw_filters", bufs=3))
+        bank_pool = stack.enter_context(tc.psum_pool(name="transposed", bufs=4))
+        acc_pool = stack.enter_context(tc.psum_pool(name="sums", bufs=2))
+
+        identity = keep.tile([P, P], F32, name="identity")
+        zeros = keep.tile([P, C_IN * SIDE_IN], BF16, name="zeros")
+        x_sb = keep.tile([P, C_IN, SIDE_IN * SIDE_IN], BF16, name="x_sb")
+        padded = [keep.tile([P, C_IN, TAPS, ROW], BF16, name="padded%d" % b) for b in range(2)]
+        pairs = [keep.tile([P, IMAGES, 2 * PAIR_PITCH], BF16, name="pair%d" % b) for b in range(2)]
+        codes = keep.tile([P, SIDE_OUT, PASSES, SIDE_OUT * IMAGES], U32, name="codes", align_bytes=64)
+        code_scales = keep.tile([P, SIDE_OUT, PASSES, SIDE_OUT * IMAGES], U8, name="code_scales", align_bytes=64)
+        filter_scales = keep.tile(
+            [P, SIDE_OUT * GROUPS_ROW, PASSES, N_MOVING], U8, name="filter_scales", align_bytes=64
+        )
+
+        nc.sync.dma_start(out=x_sb[:], in_=x.rearrange("n c h w -> n c (h w)"))
+
+        with tc.tile_pool(name="raw_scales", bufs=1) as scale_pool:
+            raw_scales = scale_pool.tile([P, PASSES * O_CHUNK, PIXELS // 4], I32, name="raw_scales")
+            nc.vector.memset(raw_scales[:], 0)
+            for chunk in range(CHUNKS):
+                groups = slice(PASSES * O_CHUNK * chunk, PASSES * O_CHUNK * (chunk + 1))
+                for quadrant in range(4):
+                    first = 32 * quadrant + 4 * chunk
+                    nc.sync.dma_start(
+                        out=raw_scales[first : first + 4, :, :],
+                        in_=filters_scales[groups, 4 * quadrant : 4 * quadrant + 4, :]
+                        .rearrange("g r n -> r g n")
+                        .bitcast(I32),
+                    )
+            nc.vector.tensor_copy(
+                out=filter_scales[:].bitcast(I32),
+                in_=raw_scales[:].rearrange("p (o f) g -> p g f o", f=PASSES),
+            )
+
+        for b in range(2):
+            nc.vector.memset(padded[b][:].bitcast(I32), 0)
+        nc.vector.memset(zeros[:].bitcast(I32), 0)
+        for b in range(2):
+            nc.vector.memset(pairs[b][:].bitcast(I32), 0)
+        make_identity(nc, identity[:])
+
+        grouped_pool = stack.enter_context(tc.tile_pool(name="grouped", bufs=2))
+        moving_pool = stack.enter_context(tc.tile_pool(name="moving", bufs=2))
+        bias_pool = stack.enter_context(tc.tile_pool(name="bias", bufs=3))
+        out_pool = stack.enter_context(tc.tile_pool(name="result", bufs=3))
+
+        def load_filters(chunk):
+            raw = raw_pool.tile([P, PASSES * O_CHUNK, PIXELS], I32, name="raw")
+            groups = slice(PASSES * O_CHUNK * chunk, PASSES * O_CHUNK * (chunk + 1))
+            nc.sync.dma_start(
+                out=raw[:], in_=filters_words[groups].rearrange("g p n t -> p g (n t)").bitcast(I32)
+            )
+            return raw
+
+        def pad_row(h):
+            tile = padded[h % 2]
+            first = 1 if h == 0 else 0
+            last = TAPS - 1 if h == SIDE_OUT - 1 else TAPS
+            top = h + first - 1
+            nc.scalar.copy(
+                out=tile[:, :, first:last, 1:ROW],
+                in_=x_sb[:, :, SIDE_IN * top : SIDE_IN * (top + last - first)].rearrange(
+                    "p c (i w) -> p c i w", w=SIDE_IN
+                ),
+            )
+            if last < TAPS:
+                nc.scalar.copy(out=tile[:, :, last, 1:ROW], in_=zeros[:].rearrange("p (c w) -> p c w", w=SIDE_IN))
+
+        def transpose_pair(pair):
+            words = pairs[pair % 2][:].bitcast(F32)
+            for bank in range(PAIR_WORDS // BANK_PLANES):
+                planes = bank_pool.tile([P, BANK_PLANES, IMAGES], F32, name="planes")
+                for m in range(BANK_PLANES):
+                    plane = BANK_PLANES * bank + m
+                    row, rest = divmod(plane, PASSES * ROW_WORDS)
+                    f, a = divmod(rest, ROW_WORDS)
+                    source = padded[row][:].bitcast(F32).rearrange("p c i a -> p (c i) a")
+                    nc.tensor.transpose(planes[:, m, :], source[:, P * f : P * (f + 1), a], identity[:])
+                nc.scalar.copy(
+                    out=words[:, :, BANK_PLANES * bank : BANK_PLANES * (bank + 1)],
+                    in_=planes[:].rearrange("p a n -> p n a"),
+                )
+
+        def quantise_row(h):
+            values = pairs[(h // 2) % 2]
+            tiles = []
+            for f in range(PASSES):
+                grouped = grouped_pool.tile([P, SIDE_OUT, IMAGES, TAPS], BF16, name="grouped", align_bytes=64)
+                start = ROW * (PASSES * (h % 2) + f)
+                for s in range(TAPS):
+                    if s % 2 == 0:
+                        nc.scalar.copy(
+                            out=grouped[:].bitcast(F32)[:, s:SIDE_OUT:TAPS, :, :],
+                            in_=values[:]
+                            .bitcast(F32)[:, :, (start + s) // 2 : (start + s) // 2 + TAPS]
+                            .rearrange("p n (b u) -> p b n u", u=2),
+                        )
+                    else:
+                        nc.vector.tensor_copy(
+                            out=grouped[:, s:SIDE_OUT:TAPS, :, :],
+                            in_=values[:, :, start + s : start + s + 2 * TAPS].rearrange(
+                                "p n (b j) -> p b n j", j=TAPS
+                            ),
+                        )
+                tiles.append(grouped)
+            for f in range(PASSES):
+                nc.vector.quantize_mx(
+                    out=codes[:, h, f, :].bitcast(FP8X4),
+                    scales=code_scales[:, h, f, :],
+                    in_=tiles[f][:].rearrange("p w n j -> p (w n j)"),
+                )
+
+        def multiply(chunk, h, raw, bias_sb, result):
+            moving = moving_pool.tile([P, GROUPS_ROW, PASSES, N_MOVING], I32, name="moving", align_bytes=64)
+            nc.vector.tensor_copy(
+                out=moving[:].rearrange("p g f (o q) -> p g f o q", q=PX_GROUP),
+                in_=raw[:]
+                .rearrange("p (o f) n -> p o f n", f=PASSES)[:, :, :, SIDE_OUT * h : SIDE_OUT * (h + 1)]
+                .rearrange("p o f (g q) -> p g f o q", q=PX_GROUP),
+            )
+            sums = acc_pool.tile([P, GROUPS_ROW * BANK], F32, name="sums")
+            for g in range(GROUPS_ROW):
+                for q in range(PX_GROUP):
+                    w = PX_GROUP * g + q
+                    images = slice(IMAGES * w, IMAGES * (w + 1))
+                    for f in range(PASSES):
+                        nc.tensor.matmul_mx(
+                            out=sums[:, BANK * g + N_MOVING * q : BANK * g + N_MOVING * (q + 1)],
+                            lhsT=codes[:, h, f, images].bitcast(FP8X4),
+                            lhsT_scale=code_scales[:, h, f, images],
+                            rhs=moving[:, g, f, :].bitcast(FP8X4),
+                            rhs_scale=filter_scales[4 * chunk : P, GROUPS_ROW * h + g, f, :],
+                            start=(f == 0),
+                            stop=(f == PASSES - 1),
+                        )
+            flat = sums
+            step = N_MOVING + 1
+            for g in range(GROUPS_ROW):
+                if g == 0:
+                    own = flat[:, 0 : PX_GROUP * step].rearrange("p (q r) -> p q r", r=step)[:, :, 0 : N_MOVING - 3 : PX_GROUP]
+                else:
+                    own = flat[:, 2 * BANK - PX_GROUP * step : 2 * BANK].rearrange("p (q r) -> p q r", r=step)[:, :, PX_GROUP : step : PX_GROUP]
+                pixels = slice(SIDE_OUT * h + PX_GROUP * g, SIDE_OUT * h + PX_GROUP * (g + 1))
+                nc.vector.tensor_tensor(
+                    out=result[:, :, pixels],
+                    in0=own.rearrange("p q o -> p o q"),
+                    in1=bias_sb[:, :, pixels],
+                    op=mybir.AluOpType.add,
+                )
+
+        raws = {}
+        biases = {}
+        results = {}
+        for chunk in range(3):
+            raws[chunk] = load_filters(chunk)
+
+        pad_row(0)
+        pad_row(1)
+        transpose_pair(0)
+        for step_no in range(SIDE_OUT + LAG * (CHUNKS - 1)):
+            if step_no + 2 < SIDE_OUT:
+                pad_row(step_no + 2)
+            if step_no < SIDE_OUT:
+                quantise_row(step_no)
+            if step_no % 2 == 1 and step_no + 1 < SIDE_OUT:
+                transpose_pair((step_no + 1) // 2)
+            for chunk in range(CHUNKS):
+                h = step_no - LAG * chunk
+                if 0 <= h < SIDE_OUT:
+                    channels = slice(O_CHUNK * chunk, O_CHUNK * (chunk + 1))
+                    if h == 0:
+                        if chunk not in raws:
+                            raws[chunk] = load_filters(chunk)
+                        bias_sb = bias_pool.tile([P, O_CHUNK, PIXELS], BF16, name="bias_sb")
+                        nc.scalar.dma_start(
+                            out=bias_sb[:].rearrange("p o n -> p (o n)"),
+                            in_=bias[channels, :].rearrange("o n -> (o n)").partition_broadcast(P),
+                        )
+                        biases[chunk] = bias_sb
+                        result = out_pool.tile([P, O_CHUNK, PIXELS], F32, name="result")
+                        results[chunk] = result
+                    multiply(chunk, h, raws[chunk], biases[chunk], results[chunk])
+                    if h == SIDE_OUT - 1:
+                        nc.scalar.dma_start(
+                            out=out[:, channels, :, :].rearrange("n o h w -> n o (h w)"), in_=results[chunk][:]
+                        )

@@ -19,7 +19,6 @@ TAPS = 4
 C_OUT = 128
 PIXELS = SIDE_OUT * SIDE_OUT
 PASSES = 2
-CH_PASS = C_IN // PASSES
 ROW = SIDE_IN + 1
 ROW_WORDS = ROW // 2
 PAIR_WORDS = 2 * PASSES * ROW_WORDS
@@ -27,11 +26,13 @@ PAIR_PITCH = 24
 BANK_PLANES = 4
 O_CHUNK = 32
 CHUNKS = C_OUT // O_CHUNK
+CHUNK_GROUPS = PASSES * O_CHUNK
 PX_GROUP = 4
 GROUPS_ROW = SIDE_OUT // PX_GROUP
 N_MOVING = O_CHUNK * PX_GROUP
 BANK = 512
-LAG = 3
+LAG = 2
+EARLY_STEPS = 6
 
 FLOPS = 2 * IMAGES * C_IN * TAPS * TAPS * C_OUT * PIXELS
 
@@ -41,189 +42,247 @@ def tile_localconv2dlayer_e_kernel(tc, x, filters_words, filters_scales, bias, o
     with ExitStack() as stack:
         keep = stack.enter_context(tc.tile_pool(name="keep", bufs=1))
         raw_pool = stack.enter_context(tc.tile_pool(name="raw_filters", bufs=3))
-        bank_pool = stack.enter_context(tc.psum_pool(name="transposed", bufs=4))
-        acc_pool = stack.enter_context(tc.psum_pool(name="sums", bufs=2))
-
-        identity = keep.tile([P, P], F32, name="identity")
-        zeros = keep.tile([P, C_IN * SIDE_IN], BF16, name="zeros")
-        x_sb = keep.tile([P, C_IN, SIDE_IN * SIDE_IN], BF16, name="x_sb")
-        padded = [keep.tile([P, C_IN, TAPS, ROW], BF16, name="padded%d" % b) for b in range(2)]
-        pairs = [keep.tile([P, IMAGES, 2 * PAIR_PITCH], BF16, name="pair%d" % b) for b in range(2)]
-        codes = keep.tile([P, SIDE_OUT, PASSES, SIDE_OUT * IMAGES], U32, name="codes", align_bytes=64)
-        code_scales = keep.tile([P, SIDE_OUT, PASSES, SIDE_OUT * IMAGES], U8, name="code_scales", align_bytes=64)
-        filter_scales = keep.tile(
-            [P, SIDE_OUT * GROUPS_ROW, PASSES, N_MOVING], U8, name="filter_scales", align_bytes=64
-        )
-
-        nc.sync.dma_start(out=x_sb[:], in_=x.rearrange("n c h w -> n c (h w)"))
-
-        with tc.tile_pool(name="raw_scales", bufs=1) as scale_pool:
-            raw_scales = scale_pool.tile([P, PASSES * O_CHUNK, PIXELS // 4], I32, name="raw_scales")
-            nc.vector.memset(raw_scales[:], 0)
-            for chunk in range(CHUNKS):
-                groups = slice(PASSES * O_CHUNK * chunk, PASSES * O_CHUNK * (chunk + 1))
-                for quadrant in range(4):
-                    first = 32 * quadrant + 4 * chunk
-                    nc.sync.dma_start(
-                        out=raw_scales[first : first + 4, :, :],
-                        in_=filters_scales[groups, 4 * quadrant : 4 * quadrant + 4, :]
-                        .rearrange("g r n -> r g n")
-                        .bitcast(I32),
-                    )
-            nc.vector.tensor_copy(
-                out=filter_scales[:].bitcast(I32),
-                in_=raw_scales[:].rearrange("p (o f) g -> p g f o", f=PASSES),
-            )
-
-        for b in range(2):
-            nc.vector.memset(padded[b][:].bitcast(I32), 0)
-        nc.vector.memset(zeros[:].bitcast(I32), 0)
-        for b in range(2):
-            nc.vector.memset(pairs[b][:].bitcast(I32), 0)
-        make_identity(nc, identity[:])
-
-        grouped_pool = stack.enter_context(tc.tile_pool(name="grouped", bufs=2))
-        moving_pool = stack.enter_context(tc.tile_pool(name="moving", bufs=2))
+        moving_pool = stack.enter_context(tc.tile_pool(name="moving", bufs=3))
         bias_pool = stack.enter_context(tc.tile_pool(name="bias", bufs=3))
         out_pool = stack.enter_context(tc.tile_pool(name="result", bufs=3))
+        grouped_pool = stack.enter_context(tc.tile_pool(name="grouped", bufs=3))
+        bank_pool = stack.enter_context(tc.psum_pool(name="transposed", bufs=2))
+        acc_pool = stack.enter_context(tc.psum_pool(name="sums", bufs=3))
 
-        def load_filters(chunk):
-            raw = raw_pool.tile([P, PASSES * O_CHUNK, PIXELS], I32, name="raw")
-            groups = slice(PASSES * O_CHUNK * chunk, PASSES * O_CHUNK * (chunk + 1))
+        identity = keep.tile([P, P], F32, name="identity")
+        pairs = [keep.tile([P, IMAGES, 2 * PAIR_PITCH], BF16, name="pair%d" % b) for b in range(2)]
+        codes = keep.tile([P, SIDE_OUT, PASSES, SIDE_OUT * IMAGES], U32, name="codes", align_bytes=64)
+        code_scales = keep.tile([P, SIDE_OUT, TAPS * IMAGES], U8, name="code_scales", align_bytes=64)
+        raw_scales = keep.tile([P, CHUNK_GROUPS, PIXELS // 4], I32, name="raw_scales")
+        filter_scales = keep.tile(
+            [P, CHUNKS, SIDE_OUT * GROUPS_ROW, PASSES, N_MOVING], U8, name="filter_scales", align_bytes=64
+        )
+
+        def load_filters(chunk, pool):
+            groups = slice(CHUNK_GROUPS * chunk, CHUNK_GROUPS * (chunk + 1))
+            for quadrant in range(4):
+                nc.sync.dma_start(
+                    out=raw_scales[32 * quadrant : 32 * quadrant + 4, :, :],
+                    in_=filters_scales[groups, 4 * quadrant : 4 * quadrant + 4, :]
+                    .rearrange("g r n -> r g n")
+                    .bitcast(I32),
+                )
+            raw = pool.tile([P, CHUNK_GROUPS, PIXELS], I32, name="raw")
             nc.sync.dma_start(
                 out=raw[:], in_=filters_words[groups].rearrange("g p n t -> p g (n t)").bitcast(I32)
             )
             return raw
 
-        def pad_row(h):
-            tile = padded[h % 2]
-            first = 1 if h == 0 else 0
-            last = TAPS - 1 if h == SIDE_OUT - 1 else TAPS
-            top = h + first - 1
-            nc.scalar.copy(
-                out=tile[:, :, first:last, 1:ROW],
-                in_=x_sb[:, :, SIDE_IN * top : SIDE_IN * (top + last - first)].rearrange(
-                    "p c (i w) -> p c i w", w=SIDE_IN
-                ),
+        def spread_scales(chunk):
+            nc.vector.tensor_copy(
+                out=filter_scales[:, chunk].bitcast(I32),
+                in_=raw_scales[:].rearrange("p (o f) g -> p g f o", f=PASSES),
             )
-            if last < TAPS:
-                nc.scalar.copy(out=tile[:, :, last, 1:ROW], in_=zeros[:].rearrange("p (c w) -> p c w", w=SIDE_IN))
-
-        def transpose_pair(pair):
-            words = pairs[pair % 2][:].bitcast(F32)
-            for bank in range(PAIR_WORDS // BANK_PLANES):
-                planes = bank_pool.tile([P, BANK_PLANES, IMAGES], F32, name="planes")
-                for m in range(BANK_PLANES):
-                    plane = BANK_PLANES * bank + m
-                    row, rest = divmod(plane, PASSES * ROW_WORDS)
-                    f, a = divmod(rest, ROW_WORDS)
-                    source = padded[row][:].bitcast(F32).rearrange("p c i a -> p (c i) a")
-                    nc.tensor.transpose(planes[:, m, :], source[:, P * f : P * (f + 1), a], identity[:])
-                nc.scalar.copy(
-                    out=words[:, :, BANK_PLANES * bank : BANK_PLANES * (bank + 1)],
-                    in_=planes[:].rearrange("p a n -> p n a"),
-                )
 
         def quantise_row(h):
             values = pairs[(h // 2) % 2]
-            tiles = []
+            previous = None
             for f in range(PASSES):
-                grouped = grouped_pool.tile([P, SIDE_OUT, IMAGES, TAPS], BF16, name="grouped", align_bytes=64)
                 start = ROW * (PASSES * (h % 2) + f)
-                for s in range(TAPS):
-                    if s % 2 == 0:
-                        nc.scalar.copy(
-                            out=grouped[:].bitcast(F32)[:, s:SIDE_OUT:TAPS, :, :],
-                            in_=values[:]
-                            .bitcast(F32)[:, :, (start + s) // 2 : (start + s) // 2 + TAPS]
-                            .rearrange("p n (b u) -> p b n u", u=2),
-                        )
-                    else:
-                        nc.vector.tensor_copy(
-                            out=grouped[:, s:SIDE_OUT:TAPS, :, :],
-                            in_=values[:, :, start + s : start + s + 2 * TAPS].rearrange(
-                                "p n (b j) -> p b n j", j=TAPS
-                            ),
-                        )
-                tiles.append(grouped)
-            for f in range(PASSES):
-                nc.vector.quantize_mx(
-                    out=codes[:, h, f, :].bitcast(FP8X4),
-                    scales=code_scales[:, h, f, :],
-                    in_=tiles[f][:].rearrange("p w n j -> p (w n j)"),
-                )
+                for e in range(TAPS // 2):
+                    grouped = grouped_pool.tile([P, 2, 2, IMAGES, TAPS], BF16, name="grouped", align_bytes=64)
+                    first = start + 2 * e
+                    nc.scalar.copy(
+                        out=grouped[:].bitcast(F32)[:, 0, :, :, :],
+                        in_=values[:].bitcast(F32)[:, :, first // 2 : first // 2 + TAPS].rearrange(
+                            "p n (b u) -> p b n u", u=2
+                        ),
+                    )
+                    nc.vector.tensor_copy(
+                        out=grouped[:, 1, :, :, :],
+                        in_=values[:, :, first + 1 : first + 1 + 2 * TAPS].rearrange("p n (b j) -> p b n j", j=TAPS),
+                    )
+                    if previous is not None:
+                        quantise(h, previous)
+                    previous = (f, e, grouped)
+            quantise(h, previous)
 
-        def multiply(chunk, h, raw, bias_sb, result):
-            moving = moving_pool.tile([P, GROUPS_ROW, PASSES, N_MOVING], I32, name="moving", align_bytes=64)
-            nc.vector.tensor_copy(
-                out=moving[:].rearrange("p g f (o q) -> p g f o q", q=PX_GROUP),
-                in_=raw[:]
-                .rearrange("p (o f) n -> p o f n", f=PASSES)[:, :, :, SIDE_OUT * h : SIDE_OUT * (h + 1)]
-                .rearrange("p o f (g q) -> p g f o q", q=PX_GROUP),
+        def quantise(h, item):
+            f, e, grouped = item
+            columns = slice(TAPS * IMAGES * e, TAPS * IMAGES * (e + 1))
+            nc.vector.quantize_mx(
+                out=codes[:, h, f, columns].bitcast(FP8X4),
+                scales=code_scales[4 * (2 * f + e) : P, h, :],
+                in_=grouped[:].rearrange("p s b n j -> p (s b n j)"),
             )
-            sums = acc_pool.tile([P, GROUPS_ROW * BANK], F32, name="sums")
-            for g in range(GROUPS_ROW):
-                for q in range(PX_GROUP):
-                    w = PX_GROUP * g + q
-                    images = slice(IMAGES * w, IMAGES * (w + 1))
-                    for f in range(PASSES):
-                        nc.tensor.matmul_mx(
-                            out=sums[:, BANK * g + N_MOVING * q : BANK * g + N_MOVING * (q + 1)],
-                            lhsT=codes[:, h, f, images].bitcast(FP8X4),
-                            lhsT_scale=code_scales[:, h, f, images],
-                            rhs=moving[:, g, f, :].bitcast(FP8X4),
-                            rhs_scale=filter_scales[4 * chunk : P, GROUPS_ROW * h + g, f, :],
-                            start=(f == 0),
-                            stop=(f == PASSES - 1),
-                        )
-            flat = sums
-            step = N_MOVING + 1
-            for g in range(GROUPS_ROW):
-                if g == 0:
-                    own = flat[:, 0 : PX_GROUP * step].rearrange("p (q r) -> p q r", r=step)[:, :, 0 : N_MOVING - 3 : PX_GROUP]
-                else:
-                    own = flat[:, 2 * BANK - PX_GROUP * step : 2 * BANK].rearrange("p (q r) -> p q r", r=step)[:, :, PX_GROUP : step : PX_GROUP]
-                pixels = slice(SIDE_OUT * h + PX_GROUP * g, SIDE_OUT * h + PX_GROUP * (g + 1))
-                nc.vector.tensor_tensor(
-                    out=result[:, :, pixels],
-                    in0=own.rearrange("p q o -> p o q"),
-                    in1=bias_sb[:, :, pixels],
-                    op=mybir.AluOpType.add,
-                )
 
         raws = {}
         biases = {}
         results = {}
-        for chunk in range(3):
-            raws[chunk] = load_filters(chunk)
+        first_step = [LAG * chunk for chunk in range(CHUNKS - 1)] + [SIDE_OUT]
+        units = [
+            (chunk, step_no - first_step[chunk])
+            for step_no in range(2 * SIDE_OUT)
+            for chunk in range(CHUNKS)
+            if 0 <= step_no - first_step[chunk] < SIDE_OUT
+        ]
+        late_from = units.index((0, EARLY_STEPS))
+        movings = {}
+        sums_of = {}
 
-        pad_row(0)
-        pad_row(1)
-        transpose_pair(0)
-        for step_no in range(SIDE_OUT + LAG * (CHUNKS - 1)):
-            if step_no + 2 < SIDE_OUT:
-                pad_row(step_no + 2)
-            if step_no < SIDE_OUT:
-                quantise_row(step_no)
-            if step_no % 2 == 1 and step_no + 1 < SIDE_OUT:
-                transpose_pair((step_no + 1) // 2)
-            for chunk in range(CHUNKS):
-                h = step_no - LAG * chunk
-                if 0 <= h < SIDE_OUT:
-                    channels = slice(O_CHUNK * chunk, O_CHUNK * (chunk + 1))
-                    if h == 0:
-                        if chunk not in raws:
-                            raws[chunk] = load_filters(chunk)
-                        bias_sb = bias_pool.tile([P, O_CHUNK, PIXELS], BF16, name="bias_sb")
-                        nc.scalar.dma_start(
-                            out=bias_sb[:].rearrange("p o n -> p (o n)"),
-                            in_=bias[channels, :].rearrange("o n -> (o n)").partition_broadcast(P),
+        def open_chunk(chunk):
+            bias_sb = bias_pool.tile([P, O_CHUNK, PIXELS], BF16, name="bias_sb")
+            nc.sync.dma_start(
+                out=bias_sb[:].rearrange("p o n -> p (o n)"),
+                in_=bias[O_CHUNK * chunk : O_CHUNK * (chunk + 1), :].rearrange("o n -> (o n)").partition_broadcast(P),
+            )
+            biases[chunk] = bias_sb
+            result = out_pool.tile([P, O_CHUNK, PIXELS], F32, name="result")
+            results[chunk] = result
+
+        def regroup_filters(k):
+            chunk, h = units[k]
+            moving = moving_pool.tile([P, GROUPS_ROW, PASSES, N_MOVING], I32, name="moving", align_bytes=64)
+            nc.vector.tensor_copy(
+                out=moving[:].rearrange("p g f (o q) -> p g f o q", q=PX_GROUP),
+                in_=raws[chunk][:]
+                .rearrange("p (o f) n -> p o f n", f=PASSES)[:, :, :, SIDE_OUT * h : SIDE_OUT * (h + 1)]
+                .rearrange("p o f (g q) -> p g f o q", q=PX_GROUP),
+            )
+            movings[k] = moving
+
+        def multiply(k):
+            chunk, h = units[k]
+            moving = movings[k]
+            sums = acc_pool.tile([P, GROUPS_ROW * BANK], F32, name="sums")
+            for g in range(GROUPS_ROW):
+                for q in range(PX_GROUP):
+                    block = IMAGES * (2 * q + g)
+                    in_call = IMAGES * (2 * (q % 2) + g)
+                    for f in range(PASSES):
+                        nc.tensor.matmul_mx(
+                            out=sums[:, BANK * g + N_MOVING * q : BANK * g + N_MOVING * (q + 1)],
+                            lhsT=codes[:, h, f, block : block + IMAGES].bitcast(FP8X4),
+                            lhsT_scale=code_scales[4 * (2 * f + q // 2) : P, h, in_call : in_call + IMAGES],
+                            rhs=moving[:, g, f, :].bitcast(FP8X4),
+                            rhs_scale=filter_scales[:, chunk, GROUPS_ROW * h + g, f, :],
+                            start=(f == 0),
+                            stop=(f == PASSES - 1),
                         )
-                        biases[chunk] = bias_sb
-                        result = out_pool.tile([P, O_CHUNK, PIXELS], F32, name="result")
-                        results[chunk] = result
-                    multiply(chunk, h, raws[chunk], biases[chunk], results[chunk])
-                    if h == SIDE_OUT - 1:
-                        nc.scalar.dma_start(
-                            out=out[:, channels, :, :].rearrange("n o h w -> n o (h w)"), in_=results[chunk][:]
-                        )
+            sums_of[k] = sums
+
+        def add_bias(k):
+            chunk, h = units[k]
+            sums = sums_of[k]
+            step = N_MOVING + 1
+            for g in range(GROUPS_ROW):
+                if g == 0:
+                    own = sums[:, 0 : PX_GROUP * step].rearrange("p (q r) -> p q r", r=step)[
+                        :, :, 0 : N_MOVING - 3 : PX_GROUP
+                    ]
+                else:
+                    own = sums[:, 2 * BANK - PX_GROUP * step : 2 * BANK].rearrange("p (q r) -> p q r", r=step)[
+                        :, :, PX_GROUP:step:PX_GROUP
+                    ]
+                pixels = slice(SIDE_OUT * h + PX_GROUP * g, SIDE_OUT * h + PX_GROUP * (g + 1))
+                nc.vector.tensor_tensor(
+                    out=results[chunk][:, :, pixels],
+                    in0=own.rearrange("p q o -> p o q"),
+                    in1=biases[chunk][:, :, pixels],
+                    op=mybir.AluOpType.add,
+                )
+            if h == SIDE_OUT - 1:
+                nc.scalar.dma_start(
+                    out=out[:, O_CHUNK * chunk : O_CHUNK * (chunk + 1), :, :].rearrange("n o h w -> n o (h w)"),
+                    in_=results[chunk][:],
+                )
+                if chunk + 3 < CHUNKS:
+                    open_chunk(chunk + 3)
+
+        def run_units(first, last, produce_row):
+            for k in range(first, last):
+                chunk, h = units[k]
+                if chunk == 0:
+                    produce_row(h)
+                if k == 0:
+                    regroup_filters(k)
+                multiply(k)
+                if k + 1 < len(units):
+                    regroup_filters(k + 1)
+                if k >= 2:
+                    add_bias(k - 2)
+
+        def scales_for_next_step(h):
+            for chunk in range(1, CHUNKS):
+                if first_step[chunk] == h + 1:
+                    spread_scales(chunk)
+                    if chunk + 1 < CHUNKS - 1:
+                        raws[chunk + 1] = load_filters(chunk + 1, raw_pool)
+                        open_chunk(chunk + 1)
+
+        stack.enter_context(tc.manual_schedule())
+        with tc.tile_pool(name="early", bufs=1) as early:
+            x_sb = early.tile([P, C_IN, SIDE_IN * SIDE_IN], BF16, name="x_sb")
+            zeros = early.tile([P, C_IN * SIDE_IN], BF16, name="zeros")
+            padded = [early.tile([P, C_IN, TAPS, ROW], BF16, name="padded%d" % b) for b in range(2)]
+
+            def pad_row(h, copy):
+                tile = padded[h % 2]
+                first = 1 if h == 0 else 0
+                last = TAPS - 1 if h == SIDE_OUT - 1 else TAPS
+                top = h + first - 1
+                copy(
+                    out=tile[:, :, first:last, 1:ROW],
+                    in_=x_sb[:, :, SIDE_IN * top : SIDE_IN * (top + last - first)].rearrange(
+                        "p c (i w) -> p c i w", w=SIDE_IN
+                    ),
+                )
+                if last < TAPS:
+                    copy(out=tile[:, :, last, 1:ROW], in_=zeros[:].rearrange("p (c w) -> p c w", w=SIDE_IN))
+
+            def transpose_pair(pair):
+                words = pairs[pair % 2][:].bitcast(F32)
+                for bank in range(PAIR_WORDS // BANK_PLANES):
+                    planes = bank_pool.tile([P, BANK_PLANES, IMAGES], F32, name="planes")
+                    for m in range(BANK_PLANES):
+                        row, rest = divmod(BANK_PLANES * bank + m, PASSES * ROW_WORDS)
+                        f, a = divmod(rest, ROW_WORDS)
+                        source = padded[row][:].bitcast(F32).rearrange("p c i a -> p (c i) a")
+                        nc.tensor.transpose(planes[:, m, :], source[:, P * f : P * (f + 1), a], identity[:])
+                    nc.scalar.copy(
+                        out=words[:, :, BANK_PLANES * bank : BANK_PLANES * (bank + 1)],
+                        in_=planes[:].rearrange("p a n -> p n a"),
+                    )
+
+            def early_row(h):
+                quantise_row(h)
+                scales_for_next_step(h)
+                if h % 2 == 0:
+                    pad_row(h + 2, nc.scalar.copy)
+                    pad_row(h + 3, nc.scalar.copy)
+                else:
+                    transpose_pair((h + 1) // 2)
+
+            nc.sync.dma_start(out=x_sb[:], in_=x.rearrange("n c h w -> n c (h w)"))
+            nc.vector.memset(raw_scales[:], 0)
+            for b in range(2):
+                nc.vector.memset(padded[b][:].bitcast(I32), 0)
+            nc.vector.memset(zeros[:].bitcast(I32), 0)
+            make_identity(nc, identity[:])
+            for b in range(2):
+                nc.gpsimd.memset(pairs[b][:].bitcast(F32), 0.0)
+            raws[0] = load_filters(0, raw_pool)
+            open_chunk(0)
+
+            pad_row(0, nc.vector.tensor_copy)
+            pad_row(1, nc.scalar.copy)
+            transpose_pair(0)
+            spread_scales(0)
+            raws[1] = load_filters(1, raw_pool)
+            open_chunk(1)
+            run_units(0, late_from, early_row)
+
+        def late_row(h):
+            quantise_row(h)
+            scales_for_next_step(h)
+
+        with tc.tile_pool(name="late", bufs=1, reuse_waits="tile") as late:
+            raws[CHUNKS - 1] = load_filters(CHUNKS - 1, late)
+            run_units(late_from, len(units), late_row)
+            add_bias(len(units) - 2)
+            add_bias(len(units) - 1)

@@ -42,8 +42,7 @@ def tile_localconv2dlayer_e_kernel(tc, x, filters_words, filters_scales, bias, o
     with ExitStack() as stack:
         keep = stack.enter_context(tc.tile_pool(name="keep", bufs=1))
         raw_pool = stack.enter_context(tc.tile_pool(name="raw_filters", bufs=3))
-        moving_pool = stack.enter_context(tc.tile_pool(name="moving", bufs=3))
-        bias_pool = stack.enter_context(tc.tile_pool(name="bias", bufs=3))
+        moving_pool = stack.enter_context(tc.tile_pool(name="moving", bufs=2))
         out_pool = stack.enter_context(tc.tile_pool(name="result", bufs=3))
         grouped_pool = stack.enter_context(tc.tile_pool(name="grouped", bufs=3))
         bank_pool = stack.enter_context(tc.psum_pool(name="transposed", bufs=2))
@@ -53,6 +52,8 @@ def tile_localconv2dlayer_e_kernel(tc, x, filters_words, filters_scales, bias, o
         pairs = [keep.tile([P, IMAGES, 2 * PAIR_PITCH], BF16, name="pair%d" % b) for b in range(2)]
         codes = keep.tile([P, SIDE_OUT, PASSES, SIDE_OUT * IMAGES], U32, name="codes", align_bytes=64)
         code_scales = keep.tile([P, SIDE_OUT, TAPS * IMAGES], U8, name="code_scales", align_bytes=64)
+        bias_rows = keep.tile([P, PIXELS], BF16, name="bias_rows")
+        bias_all = keep.tile([P, SIDE_OUT, SIDE_OUT // 2, C_OUT, 2], BF16, name="bias_all")
         raw_scales = keep.tile([P, CHUNK_GROUPS, PIXELS // 4], I32, name="raw_scales")
         filter_scales = keep.tile(
             [P, CHUNKS, SIDE_OUT * GROUPS_ROW, PASSES, N_MOVING], U8, name="filter_scales", align_bytes=64
@@ -112,7 +113,6 @@ def tile_localconv2dlayer_e_kernel(tc, x, filters_words, filters_scales, bias, o
             )
 
         raws = {}
-        biases = {}
         results = {}
         first_step = [LAG * chunk for chunk in range(CHUNKS - 1)] + [SIDE_OUT]
         units = [
@@ -126,12 +126,6 @@ def tile_localconv2dlayer_e_kernel(tc, x, filters_words, filters_scales, bias, o
         sums_of = {}
 
         def open_chunk(chunk):
-            bias_sb = bias_pool.tile([P, O_CHUNK, PIXELS], BF16, name="bias_sb")
-            nc.sync.dma_start(
-                out=bias_sb[:].rearrange("p o n -> p (o n)"),
-                in_=bias[O_CHUNK * chunk : O_CHUNK * (chunk + 1), :].rearrange("o n -> (o n)").partition_broadcast(P),
-            )
-            biases[chunk] = bias_sb
             result = out_pool.tile([P, O_CHUNK, PIXELS], F32, name="result")
             results[chunk] = result
 
@@ -181,9 +175,11 @@ def tile_localconv2dlayer_e_kernel(tc, x, filters_words, filters_scales, bias, o
                     ]
                 pixels = slice(SIDE_OUT * h + PX_GROUP * g, SIDE_OUT * h + PX_GROUP * (g + 1))
                 nc.vector.tensor_tensor(
-                    out=results[chunk][:, :, pixels],
-                    in0=own.rearrange("p q o -> p o q"),
-                    in1=biases[chunk][:, :, pixels],
+                    out=results[chunk][:, :, pixels].rearrange("p o (a e) -> p o a e", e=2),
+                    in0=own.rearrange("p (a e) o -> p o a e", e=2),
+                    in1=bias_all[:, h, 2 * g : 2 * g + 2, O_CHUNK * chunk : O_CHUNK * (chunk + 1), :].rearrange(
+                        "p a o e -> p o a e"
+                    ),
                     op=mybir.AluOpType.add,
                 )
             if h == SIDE_OUT - 1:
@@ -248,6 +244,14 @@ def tile_localconv2dlayer_e_kernel(tc, x, filters_words, filters_scales, bias, o
                         out=words[:, :, BANK_PLANES * bank : BANK_PLANES * (bank + 1)],
                         in_=planes[:].rearrange("p a n -> p n a"),
                     )
+                for h in (2 * pair, 2 * pair + 1):
+                    planes = bank_pool.tile([P, BANK_PLANES, C_OUT], F32, name="planes")
+                    for m in range(BANK_PLANES):
+                        word = BANK_PLANES * h + m
+                        nc.tensor.transpose(
+                            planes[:, m, :], bias_rows[:].bitcast(F32)[:, word : word + 1].to_broadcast([P, P]), identity[:]
+                        )
+                    nc.scalar.copy(out=bias_all[:, h].bitcast(F32).rearrange("p a o e -> p a (o e)"), in_=planes[:])
 
             def early_row(h):
                 quantise_row(h)
@@ -259,6 +263,7 @@ def tile_localconv2dlayer_e_kernel(tc, x, filters_words, filters_scales, bias, o
                     transpose_pair((h + 1) // 2)
 
             nc.sync.dma_start(out=x_sb[:], in_=x.rearrange("n c h w -> n c (h w)"))
+            nc.scalar.dma_start(out=bias_rows[:], in_=bias)
             nc.vector.memset(raw_scales[:], 0)
             for b in range(2):
                 nc.vector.memset(padded[b][:].bitcast(I32), 0)

@@ -21,9 +21,8 @@ PIXELS = SIDE_OUT * SIDE_OUT
 PASSES = 2
 ROW = SIDE_IN + 1
 ROW_WORDS = ROW // 2
-PAIR_WORDS = 2 * PASSES * ROW_WORDS
-PAIR_PITCH = 24
 BANK_PLANES = 4
+ROW_BANKS = 3
 O_CHUNK = 32
 CHUNKS = C_OUT // O_CHUNK
 CHUNK_GROUPS = PASSES * O_CHUNK
@@ -32,7 +31,8 @@ GROUPS_ROW = SIDE_OUT // PX_GROUP
 N_MOVING = O_CHUNK * PX_GROUP
 BANK = 512
 LAG = 2
-EARLY_STEPS = 6
+CATCH_UP = 2
+ROW_TILES = PASSES * TAPS // 2
 
 FLOPS = 2 * IMAGES * C_IN * TAPS * TAPS * C_OUT * PIXELS
 
@@ -42,18 +42,18 @@ def tile_localconv2dlayer_e_kernel(tc, x, filters_words, filters_scales, bias, o
     with ExitStack() as stack:
         keep = stack.enter_context(tc.tile_pool(name="keep", bufs=1))
         raw_pool = stack.enter_context(tc.tile_pool(name="raw_filters", bufs=3))
-        moving_pool = stack.enter_context(tc.tile_pool(name="moving", bufs=2))
+        moving_pool = stack.enter_context(tc.tile_pool(name="moving", bufs=3))
+        bias_pool = stack.enter_context(tc.tile_pool(name="bias", bufs=3))
         out_pool = stack.enter_context(tc.tile_pool(name="result", bufs=3))
         grouped_pool = stack.enter_context(tc.tile_pool(name="grouped", bufs=3))
-        bank_pool = stack.enter_context(tc.psum_pool(name="transposed", bufs=2))
-        acc_pool = stack.enter_context(tc.psum_pool(name="sums", bufs=3))
+        bank_pool = stack.enter_context(tc.psum_pool(name="transposed", bufs=4))
+        acc_pool = stack.enter_context(tc.psum_pool(name="sums", bufs=2))
 
         identity = keep.tile([P, P], F32, name="identity")
-        pairs = [keep.tile([P, IMAGES, 2 * PAIR_PITCH], BF16, name="pair%d" % b) for b in range(2)]
+        zeros = keep.tile([P, C_IN * SIDE_IN], BF16, name="zeros")
+        rows = [keep.tile([P, IMAGES, 2 * ROW_BANKS * BANK_PLANES], BF16, name="row%d" % b) for b in range(2)]
         codes = keep.tile([P, SIDE_OUT, PASSES, SIDE_OUT * IMAGES], U32, name="codes", align_bytes=64)
         code_scales = keep.tile([P, SIDE_OUT, TAPS * IMAGES], U8, name="code_scales", align_bytes=64)
-        bias_rows = keep.tile([P, PIXELS], BF16, name="bias_rows")
-        bias_all = keep.tile([P, SIDE_OUT, SIDE_OUT // 2, C_OUT, 2], BF16, name="bias_all")
         raw_scales = keep.tile([P, CHUNK_GROUPS, PIXELS // 4], I32, name="raw_scales")
         filter_scales = keep.tile(
             [P, CHUNKS, SIDE_OUT * GROUPS_ROW, PASSES, N_MOVING], U8, name="filter_scales", align_bytes=64
@@ -80,28 +80,20 @@ def tile_localconv2dlayer_e_kernel(tc, x, filters_words, filters_scales, bias, o
                 in_=raw_scales[:].rearrange("p (o f) g -> p g f o", f=PASSES),
             )
 
-        def quantise_row(h):
-            values = pairs[(h // 2) % 2]
-            previous = None
-            for f in range(PASSES):
-                start = ROW * (PASSES * (h % 2) + f)
-                for e in range(TAPS // 2):
-                    grouped = grouped_pool.tile([P, 2, 2, IMAGES, TAPS], BF16, name="grouped", align_bytes=64)
-                    first = start + 2 * e
-                    nc.scalar.copy(
-                        out=grouped[:].bitcast(F32)[:, 0, :, :, :],
-                        in_=values[:].bitcast(F32)[:, :, first // 2 : first // 2 + TAPS].rearrange(
-                            "p n (b u) -> p b n u", u=2
-                        ),
-                    )
-                    nc.vector.tensor_copy(
-                        out=grouped[:, 1, :, :, :],
-                        in_=values[:, :, first + 1 : first + 1 + 2 * TAPS].rearrange("p n (b j) -> p b n j", j=TAPS),
-                    )
-                    if previous is not None:
-                        quantise(h, previous)
-                    previous = (f, e, grouped)
-            quantise(h, previous)
+        def fill_tile(h, i):
+            f, e = divmod(i, TAPS // 2)
+            values = rows[h % 2]
+            first = ROW * f + 2 * e
+            grouped = grouped_pool.tile([P, 2, 2, IMAGES, TAPS], BF16, name="grouped", align_bytes=64)
+            nc.scalar.copy(
+                out=grouped[:].bitcast(F32)[:, 0, :, :, :],
+                in_=values[:].bitcast(F32)[:, :, first // 2 : first // 2 + TAPS].rearrange("p n (b u) -> p b n u", u=2),
+            )
+            nc.vector.tensor_copy(
+                out=grouped[:, 1, :, :, :],
+                in_=values[:, :, first + 1 : first + 1 + 2 * TAPS].rearrange("p n (b j) -> p b n j", j=TAPS),
+            )
+            return (f, e, grouped)
 
         def quantise(h, item):
             f, e, grouped = item
@@ -113,19 +105,30 @@ def tile_localconv2dlayer_e_kernel(tc, x, filters_words, filters_scales, bias, o
             )
 
         raws = {}
+        biases = {}
         results = {}
         first_step = [LAG * chunk for chunk in range(CHUNKS - 1)] + [SIDE_OUT]
-        units = [
-            (chunk, step_no - first_step[chunk])
-            for step_no in range(2 * SIDE_OUT)
-            for chunk in range(CHUNKS)
-            if 0 <= step_no - first_step[chunk] < SIDE_OUT
-        ]
-        late_from = units.index((0, EARLY_STEPS))
+        steps = []
+        done = [0] * CHUNKS
+        for step_no in range(first_step[CHUNKS - 1] + SIDE_OUT // CATCH_UP):
+            jobs = []
+            for chunk in range(CHUNKS):
+                if step_no >= first_step[chunk]:
+                    upto = min(done[chunk] + CATCH_UP, step_no + 1, SIDE_OUT)
+                    jobs.extend((chunk, h) for h in range(done[chunk], upto))
+                    done[chunk] = upto
+            steps.append(jobs)
+        units = [unit for jobs in steps for unit in jobs]
         movings = {}
         sums_of = {}
 
         def open_chunk(chunk):
+            bias_sb = bias_pool.tile([P, O_CHUNK, PIXELS], BF16, name="bias_sb")
+            nc.sync.dma_start(
+                out=bias_sb[:].rearrange("p o n -> p (o n)"),
+                in_=bias[O_CHUNK * chunk : O_CHUNK * (chunk + 1), :].rearrange("o n -> (o n)").partition_broadcast(P),
+            )
+            biases[chunk] = bias_sb
             result = out_pool.tile([P, O_CHUNK, PIXELS], F32, name="result")
             results[chunk] = result
 
@@ -175,11 +178,9 @@ def tile_localconv2dlayer_e_kernel(tc, x, filters_words, filters_scales, bias, o
                     ]
                 pixels = slice(SIDE_OUT * h + PX_GROUP * g, SIDE_OUT * h + PX_GROUP * (g + 1))
                 nc.vector.tensor_tensor(
-                    out=results[chunk][:, :, pixels].rearrange("p o (a e) -> p o a e", e=2),
-                    in0=own.rearrange("p (a e) o -> p o a e", e=2),
-                    in1=bias_all[:, h, 2 * g : 2 * g + 2, O_CHUNK * chunk : O_CHUNK * (chunk + 1), :].rearrange(
-                        "p a o e -> p o a e"
-                    ),
+                    out=results[chunk][:, :, pixels],
+                    in0=own.rearrange("p q o -> p o q"),
+                    in1=biases[chunk][:, :, pixels],
                     op=mybir.AluOpType.add,
                 )
             if h == SIDE_OUT - 1:
@@ -190,22 +191,43 @@ def tile_localconv2dlayer_e_kernel(tc, x, filters_words, filters_scales, bias, o
                 if chunk + 3 < CHUNKS:
                     open_chunk(chunk + 3)
 
-        def run_units(first, last, produce_row):
-            for k in range(first, last):
-                chunk, h = units[k]
-                if chunk == 0:
-                    produce_row(h)
-                if k == 0:
-                    regroup_filters(k)
-                multiply(k)
-                if k + 1 < len(units):
-                    regroup_filters(k + 1)
-                if k >= 2:
-                    add_bias(k - 2)
+        def copy_out(h, banks):
+            words = rows[h % 2][:].bitcast(F32)
+            for bank in range(ROW_BANKS):
+                nc.scalar.copy(
+                    out=words[:, :, BANK_PLANES * bank : BANK_PLANES * (bank + 1)],
+                    in_=banks[bank][:].rearrange("p a n -> p n a"),
+                )
 
-        def scales_for_next_step(h):
+        def run_step(step_no, transpose_row, pad_row):
+            jobs = steps[step_no] if step_no >= 0 else []
+            first_unit = sum(len(earlier) for earlier in steps[: max(step_no, 0)])
+            row = step_no + 1
+            previous = None
+            banks = None
+            for i in range(max(ROW_TILES, len(jobs))):
+                if row < SIDE_OUT and i < ROW_TILES:
+                    filled = fill_tile(row, i)
+                    if previous is not None:
+                        quantise(row, previous)
+                    previous = filled
+                if i < len(jobs):
+                    k = first_unit + i
+                    multiply(k)
+                    if k + 1 < len(units):
+                        regroup_filters(k + 1)
+                    if k >= 1:
+                        add_bias(k - 1)
+                if i == 0 and row + 1 < SIDE_OUT:
+                    banks = transpose_row(row + 1)
+            if previous is not None:
+                quantise(row, previous)
+            if banks is not None:
+                copy_out(row + 1, banks)
+            if row + 2 < SIDE_OUT:
+                pad_row(row + 2, nc.scalar.copy)
             for chunk in range(1, CHUNKS):
-                if first_step[chunk] == h + 1:
+                if first_step[chunk] == row:
                     spread_scales(chunk)
                     if chunk + 1 < CHUNKS - 1:
                         raws[chunk + 1] = load_filters(chunk + 1, raw_pool)
@@ -214,7 +236,6 @@ def tile_localconv2dlayer_e_kernel(tc, x, filters_words, filters_scales, bias, o
         stack.enter_context(tc.manual_schedule())
         with tc.tile_pool(name="early", bufs=1) as early:
             x_sb = early.tile([P, C_IN, SIDE_IN * SIDE_IN], BF16, name="x_sb")
-            zeros = early.tile([P, C_IN * SIDE_IN], BF16, name="zeros")
             padded = [early.tile([P, C_IN, TAPS, ROW], BF16, name="padded%d" % b) for b in range(2)]
 
             def pad_row(h, copy):
@@ -231,63 +252,42 @@ def tile_localconv2dlayer_e_kernel(tc, x, filters_words, filters_scales, bias, o
                 if last < TAPS:
                     copy(out=tile[:, :, last, 1:ROW], in_=zeros[:].rearrange("p (c w) -> p c w", w=SIDE_IN))
 
-            def transpose_pair(pair):
-                words = pairs[pair % 2][:].bitcast(F32)
-                for bank in range(PAIR_WORDS // BANK_PLANES):
+            def transpose_row(h):
+                source = padded[h % 2][:].bitcast(F32).rearrange("p c i a -> p (c i) a")
+                banks = []
+                for bank in range(ROW_BANKS):
                     planes = bank_pool.tile([P, BANK_PLANES, IMAGES], F32, name="planes")
                     for m in range(BANK_PLANES):
-                        row, rest = divmod(BANK_PLANES * bank + m, PASSES * ROW_WORDS)
-                        f, a = divmod(rest, ROW_WORDS)
-                        source = padded[row][:].bitcast(F32).rearrange("p c i a -> p (c i) a")
-                        nc.tensor.transpose(planes[:, m, :], source[:, P * f : P * (f + 1), a], identity[:])
-                    nc.scalar.copy(
-                        out=words[:, :, BANK_PLANES * bank : BANK_PLANES * (bank + 1)],
-                        in_=planes[:].rearrange("p a n -> p n a"),
-                    )
-                for h in (2 * pair, 2 * pair + 1):
-                    planes = bank_pool.tile([P, BANK_PLANES, C_OUT], F32, name="planes")
-                    for m in range(BANK_PLANES):
-                        word = BANK_PLANES * h + m
-                        nc.tensor.transpose(
-                            planes[:, m, :], bias_rows[:].bitcast(F32)[:, word : word + 1].to_broadcast([P, P]), identity[:]
-                        )
-                    nc.scalar.copy(out=bias_all[:, h].bitcast(F32).rearrange("p a o e -> p a (o e)"), in_=planes[:])
-
-            def early_row(h):
-                quantise_row(h)
-                scales_for_next_step(h)
-                if h % 2 == 0:
-                    pad_row(h + 2, nc.scalar.copy)
-                    pad_row(h + 3, nc.scalar.copy)
-                else:
-                    transpose_pair((h + 1) // 2)
+                        f, a = divmod(BANK_PLANES * bank + m, ROW_WORDS)
+                        if f < PASSES:
+                            nc.tensor.transpose(planes[:, m, :], source[:, P * f : P * (f + 1), a], identity[:])
+                        else:
+                            nc.tensor.transpose(planes[:, m, :], zeros[:].bitcast(F32)[:, 0:P], identity[:])
+                    banks.append(planes)
+                return banks
 
             nc.sync.dma_start(out=x_sb[:], in_=x.rearrange("n c h w -> n c (h w)"))
-            nc.scalar.dma_start(out=bias_rows[:], in_=bias)
             nc.vector.memset(raw_scales[:], 0)
             for b in range(2):
                 nc.vector.memset(padded[b][:].bitcast(I32), 0)
             nc.vector.memset(zeros[:].bitcast(I32), 0)
             make_identity(nc, identity[:])
-            for b in range(2):
-                nc.gpsimd.memset(pairs[b][:].bitcast(F32), 0.0)
             raws[0] = load_filters(0, raw_pool)
             open_chunk(0)
 
             pad_row(0, nc.vector.tensor_copy)
             pad_row(1, nc.scalar.copy)
-            transpose_pair(0)
+            copy_out(0, transpose_row(0))
             spread_scales(0)
             raws[1] = load_filters(1, raw_pool)
             open_chunk(1)
-            run_units(0, late_from, early_row)
-
-        def late_row(h):
-            quantise_row(h)
-            scales_for_next_step(h)
+            run_step(-1, transpose_row, pad_row)
+            regroup_filters(0)
+            for step_no in range(SIDE_OUT - 2):
+                run_step(step_no, transpose_row, pad_row)
 
         with tc.tile_pool(name="late", bufs=1, reuse_waits="tile") as late:
             raws[CHUNKS - 1] = load_filters(CHUNKS - 1, late)
-            run_units(late_from, len(units), late_row)
-            add_bias(len(units) - 2)
+            for step_no in range(SIDE_OUT - 2, len(steps)):
+                run_step(step_no, None, None)
             add_bias(len(units) - 1)

@@ -41,8 +41,8 @@ def tile_localconv2dlayer_e_kernel(tc, x, filters_words, filters_scales, bias, o
     nc = tc.nc
     with ExitStack() as stack:
         keep = stack.enter_context(tc.tile_pool(name="keep", bufs=1))
-        raw_pool = stack.enter_context(tc.tile_pool(name="raw_filters", bufs=3))
-        moving_pool = stack.enter_context(tc.tile_pool(name="moving", bufs=3))
+        raw_pool = stack.enter_context(tc.tile_pool(name="raw_filters", bufs=CHUNKS))
+        moving_pool = stack.enter_context(tc.tile_pool(name="moving", bufs=2))
         bias_pool = stack.enter_context(tc.tile_pool(name="bias", bufs=3))
         out_pool = stack.enter_context(tc.tile_pool(name="result", bufs=3))
         grouped_pool = stack.enter_context(tc.tile_pool(name="grouped", bufs=3))
@@ -50,7 +50,7 @@ def tile_localconv2dlayer_e_kernel(tc, x, filters_words, filters_scales, bias, o
         acc_pool = stack.enter_context(tc.psum_pool(name="sums", bufs=2))
 
         identity = keep.tile([P, P], F32, name="identity")
-        zeros = keep.tile([P, C_IN * SIDE_IN], BF16, name="zeros")
+        zeros = keep.tile([P, 2 * P], BF16, name="zeros")
         rows = [keep.tile([P, IMAGES, 2 * ROW_BANKS * BANK_PLANES], BF16, name="row%d" % b) for b in range(2)]
         codes = keep.tile([P, SIDE_OUT, PASSES, SIDE_OUT * IMAGES], U32, name="codes", align_bytes=64)
         code_scales = keep.tile([P, SIDE_OUT, TAPS * IMAGES], U8, name="code_scales", align_bytes=64)
@@ -59,7 +59,9 @@ def tile_localconv2dlayer_e_kernel(tc, x, filters_words, filters_scales, bias, o
             [P, CHUNKS, SIDE_OUT * GROUPS_ROW, PASSES, N_MOVING], U8, name="filter_scales", align_bytes=64
         )
 
-        def load_filters(chunk, pool):
+        raws = {}
+
+        def load_filters(chunk):
             groups = slice(CHUNK_GROUPS * chunk, CHUNK_GROUPS * (chunk + 1))
             for quadrant in range(4):
                 nc.sync.dma_start(
@@ -68,11 +70,11 @@ def tile_localconv2dlayer_e_kernel(tc, x, filters_words, filters_scales, bias, o
                     .rearrange("g r n -> r g n")
                     .bitcast(I32),
                 )
-            raw = pool.tile([P, CHUNK_GROUPS, PIXELS], I32, name="raw")
+            raw = raw_pool.tile([P, CHUNK_GROUPS, PIXELS], I32, name="raw")
             nc.sync.dma_start(
                 out=raw[:], in_=filters_words[groups].rearrange("g p n t -> p g (n t)").bitcast(I32)
             )
-            return raw
+            raws[chunk] = raw
 
         def spread_scales(chunk):
             nc.vector.tensor_copy(
@@ -104,10 +106,9 @@ def tile_localconv2dlayer_e_kernel(tc, x, filters_words, filters_scales, bias, o
                 in_=grouped[:].rearrange("p s b n j -> p (s b n j)"),
             )
 
-        raws = {}
         biases = {}
         results = {}
-        first_step = [LAG * chunk for chunk in range(CHUNKS - 1)] + [SIDE_OUT]
+        first_step = [LAG * chunk for chunk in range(CHUNKS)]
         steps = []
         done = [0] * CHUNKS
         for step_no in range(first_step[CHUNKS - 1] + SIDE_OUT // CATCH_UP):
@@ -122,14 +123,14 @@ def tile_localconv2dlayer_e_kernel(tc, x, filters_words, filters_scales, bias, o
         movings = {}
         sums_of = {}
 
-        def open_chunk(chunk):
-            bias_sb = bias_pool.tile([P, O_CHUNK, PIXELS], BF16, name="bias_sb")
+        def open_chunk(chunk, bias_from, result_from):
+            bias_sb = bias_from.tile([P, O_CHUNK, PIXELS], BF16, name="bias_sb")
             nc.sync.dma_start(
                 out=bias_sb[:].rearrange("p o n -> p (o n)"),
                 in_=bias[O_CHUNK * chunk : O_CHUNK * (chunk + 1), :].rearrange("o n -> (o n)").partition_broadcast(P),
             )
             biases[chunk] = bias_sb
-            result = out_pool.tile([P, O_CHUNK, PIXELS], F32, name="result")
+            result = result_from.tile([P, O_CHUNK, PIXELS], F32, name="result")
             results[chunk] = result
 
         def regroup_filters(k):
@@ -188,8 +189,6 @@ def tile_localconv2dlayer_e_kernel(tc, x, filters_words, filters_scales, bias, o
                     out=out[:, O_CHUNK * chunk : O_CHUNK * (chunk + 1), :, :].rearrange("n o h w -> n o (h w)"),
                     in_=results[chunk][:],
                 )
-                if chunk + 3 < CHUNKS:
-                    open_chunk(chunk + 3)
 
         def copy_out(h, banks):
             words = rows[h % 2][:].bitcast(F32)
@@ -225,20 +224,22 @@ def tile_localconv2dlayer_e_kernel(tc, x, filters_words, filters_scales, bias, o
             if banks is not None:
                 copy_out(row + 1, banks)
             if row + 2 < SIDE_OUT:
-                pad_row(row + 2, nc.scalar.copy)
+                pad_row(row + 2)
             for chunk in range(1, CHUNKS):
                 if first_step[chunk] == row:
                     spread_scales(chunk)
+                    if chunk + 1 < CHUNKS:
+                        load_filters(chunk + 1)
                     if chunk + 1 < CHUNKS - 1:
-                        raws[chunk + 1] = load_filters(chunk + 1, raw_pool)
-                        open_chunk(chunk + 1)
+                        open_chunk(chunk + 1, bias_pool, out_pool)
 
         stack.enter_context(tc.manual_schedule())
         with tc.tile_pool(name="early", bufs=1) as early:
             x_sb = early.tile([P, C_IN, SIDE_IN * SIDE_IN], BF16, name="x_sb")
             padded = [early.tile([P, C_IN, TAPS, ROW], BF16, name="padded%d" % b) for b in range(2)]
 
-            def pad_row(h, copy):
+            def pad_row(h):
+                copy = nc.vector.tensor_copy if h % 2 == 0 else nc.scalar.copy
                 tile = padded[h % 2]
                 first = 1 if h == 0 else 0
                 last = TAPS - 1 if h == SIDE_OUT - 1 else TAPS
@@ -250,7 +251,7 @@ def tile_localconv2dlayer_e_kernel(tc, x, filters_words, filters_scales, bias, o
                     ),
                 )
                 if last < TAPS:
-                    copy(out=tile[:, :, last, 1:ROW], in_=zeros[:].rearrange("p (c w) -> p c w", w=SIDE_IN))
+                    copy(out=tile[:, :, last, 1:ROW], in_=zeros[:, 0:SIDE_IN].unsqueeze(1).to_broadcast([P, C_IN, SIDE_IN]))
 
             def transpose_row(h):
                 source = padded[h % 2][:].bitcast(F32).rearrange("p c i a -> p (c i) a")
@@ -262,7 +263,7 @@ def tile_localconv2dlayer_e_kernel(tc, x, filters_words, filters_scales, bias, o
                         if f < PASSES:
                             nc.tensor.transpose(planes[:, m, :], source[:, P * f : P * (f + 1), a], identity[:])
                         else:
-                            nc.tensor.transpose(planes[:, m, :], zeros[:].bitcast(F32)[:, 0:P], identity[:])
+                            nc.tensor.transpose(planes[:, m, :], zeros[:].bitcast(F32), identity[:])
                     banks.append(planes)
                 return banks
 
@@ -272,22 +273,22 @@ def tile_localconv2dlayer_e_kernel(tc, x, filters_words, filters_scales, bias, o
                 nc.vector.memset(padded[b][:].bitcast(I32), 0)
             nc.vector.memset(zeros[:].bitcast(I32), 0)
             make_identity(nc, identity[:])
-            raws[0] = load_filters(0, raw_pool)
-            open_chunk(0)
+            load_filters(0)
+            open_chunk(0, bias_pool, out_pool)
 
-            pad_row(0, nc.vector.tensor_copy)
-            pad_row(1, nc.scalar.copy)
+            pad_row(0)
+            pad_row(1)
             copy_out(0, transpose_row(0))
             spread_scales(0)
-            raws[1] = load_filters(1, raw_pool)
-            open_chunk(1)
+            load_filters(1)
+            open_chunk(1, bias_pool, out_pool)
             run_step(-1, transpose_row, pad_row)
             regroup_filters(0)
             for step_no in range(SIDE_OUT - 2):
                 run_step(step_no, transpose_row, pad_row)
 
         with tc.tile_pool(name="late", bufs=1, reuse_waits="tile") as late:
-            raws[CHUNKS - 1] = load_filters(CHUNKS - 1, late)
+            open_chunk(CHUNKS - 1, late, late)
             for step_no in range(SIDE_OUT - 2, len(steps)):
                 run_step(step_no, None, None)
             add_bias(len(units) - 1)

@@ -239,19 +239,27 @@ def tile_localconv2dlayer_e_kernel(tc, x, filters_words, filters_scales, bias, o
             padded = [early.tile([P, C_IN, TAPS, ROW], BF16, name="padded%d" % b) for b in range(2)]
 
             def pad_row(h):
-                copy = nc.vector.tensor_copy if h % 2 == 0 else nc.scalar.copy
                 tile = padded[h % 2]
-                first = 1 if h == 0 else 0
-                last = TAPS - 1 if h == SIDE_OUT - 1 else TAPS
-                top = h + first - 1
-                copy(
-                    out=tile[:, :, first:last, 1:ROW],
-                    in_=x_sb[:, :, SIDE_IN * top : SIDE_IN * (top + last - first)].rearrange(
-                        "p c (i w) -> p c i w", w=SIDE_IN
-                    ),
+                if h == 0:
+                    nc.vector.tensor_copy(
+                        out=tile[:, :, 1:TAPS, 1:ROW],
+                        in_=x_sb[:, :, 0 : SIDE_IN * (TAPS - 1)].rearrange("p c (i w) -> p c i w", w=SIDE_IN),
+                    )
+                    return
+                nc.scalar.copy(
+                    out=tile[:].bitcast(F32)[:, :, 0 : TAPS - 1, :],
+                    in_=padded[(h - 1) % 2][:].bitcast(F32)[:, :, 1:TAPS, :],
                 )
-                if last < TAPS:
-                    copy(out=tile[:, :, last, 1:ROW], in_=zeros[:, 0:SIDE_IN].unsqueeze(1).to_broadcast([P, C_IN, SIDE_IN]))
+                bottom = h + TAPS - 2
+                if bottom < SIDE_IN:
+                    nc.scalar.copy(
+                        out=tile[:, :, TAPS - 1, 1:ROW], in_=x_sb[:, :, SIDE_IN * bottom : SIDE_IN * (bottom + 1)]
+                    )
+                else:
+                    nc.scalar.copy(
+                        out=tile[:, :, TAPS - 1, 1:ROW],
+                        in_=zeros[:, 0:SIDE_IN].unsqueeze(1).to_broadcast([P, C_IN, SIDE_IN]),
+                    )
 
             def transpose_row(h):
                 source = padded[h % 2][:].bitcast(F32).rearrange("p c i a -> p (c i) a")

@@ -91,7 +91,8 @@ def tile_localconv2dlayer_e_kernel(tc, x, filters_words, filters_scales, bias, o
                 out=grouped[:].bitcast(F32)[:, 0, :, :, :],
                 in_=values[:].bitcast(F32)[:, :, first // 2 : first // 2 + TAPS].rearrange("p n (b u) -> p b n u", u=2),
             )
-            nc.vector.tensor_copy(
+            odd_copy = nc.scalar.copy if i == ROW_TILES - 1 else nc.vector.tensor_copy
+            odd_copy(
                 out=grouped[:, 1, :, :, :],
                 in_=values[:, :, first + 1 : first + 1 + 2 * TAPS].rearrange("p n (b j) -> p b n j", j=TAPS),
             )

@@ -33,6 +33,9 @@ BANK = 512
 LAG = 2
 CATCH_UP = 2
 ROW_TILES = PASSES * TAPS // 2
+X_STEPS = SIDE_OUT - 4
+
+X_HALVES = (slice(0, C_IN // PASSES), slice(C_IN // PASSES, C_IN))
 
 FLOPS = 2 * IMAGES * C_IN * TAPS * TAPS * C_OUT * PIXELS
 
@@ -52,20 +55,27 @@ def tile_localconv2dlayer_e_kernel(tc, x, filters_words, filters_scales, bias, o
         identity = keep.tile([P, P], F32, name="identity")
         zeros = keep.tile([P, 2 * P], BF16, name="zeros")
         rows = [keep.tile([P, IMAGES, 2 * ROW_BANKS * BANK_PLANES], BF16, name="row%d" % b) for b in range(2)]
+        padded = [keep.tile([P, C_IN, TAPS, ROW], BF16, name="padded%d" % b) for b in range(2)]
         codes = keep.tile([P, SIDE_OUT, PASSES, SIDE_OUT * IMAGES], U32, name="codes", align_bytes=64)
         code_scales = keep.tile([P, SIDE_OUT, TAPS * IMAGES], U8, name="code_scales", align_bytes=64)
-        raw_scales = keep.tile([P, CHUNK_GROUPS, PIXELS // 4], I32, name="raw_scales")
         filter_scales = keep.tile(
             [P, CHUNKS, SIDE_OUT * GROUPS_ROW, PASSES, N_MOVING], U8, name="filter_scales", align_bytes=64
         )
 
         raws = {}
 
+        def raw_scales(chunk, partitions):
+            return (
+                codes[partitions, SIDE_OUT - 2 + chunk // PASSES, chunk % PASSES, :]
+                .bitcast(I32)
+                .rearrange("p (g w) -> p g w", w=PIXELS // 4)
+            )
+
         def load_filters(chunk):
             groups = slice(CHUNK_GROUPS * chunk, CHUNK_GROUPS * (chunk + 1))
             for quadrant in range(4):
                 nc.sync.dma_start(
-                    out=raw_scales[32 * quadrant : 32 * quadrant + 4, :, :],
+                    out=raw_scales(chunk, slice(32 * quadrant, 32 * quadrant + 4)),
                     in_=filters_scales[groups, 4 * quadrant : 4 * quadrant + 4, :]
                     .rearrange("g r n -> r g n")
                     .bitcast(I32),
@@ -79,7 +89,7 @@ def tile_localconv2dlayer_e_kernel(tc, x, filters_words, filters_scales, bias, o
         def spread_scales(chunk):
             nc.vector.tensor_copy(
                 out=filter_scales[:, chunk].bitcast(I32),
-                in_=raw_scales[:].rearrange("p (o f) g -> p g f o", f=PASSES),
+                in_=raw_scales(chunk, slice(0, P)).rearrange("p (o f) g -> p g f o", f=PASSES),
             )
 
         def fill_tile(h, i):
@@ -110,6 +120,7 @@ def tile_localconv2dlayer_e_kernel(tc, x, filters_words, filters_scales, bias, o
         biases = {}
         results = {}
         first_step = [LAG * chunk for chunk in range(CHUNKS)]
+        first_step[CHUNKS - 1] -= 1
         steps = []
         done = [0] * CHUNKS
         for step_no in range(first_step[CHUNKS - 1] + SIDE_OUT // CATCH_UP):
@@ -229,23 +240,19 @@ def tile_localconv2dlayer_e_kernel(tc, x, filters_words, filters_scales, bias, o
             for chunk in range(1, CHUNKS):
                 if first_step[chunk] == row:
                     spread_scales(chunk)
-                    if chunk + 1 < CHUNKS:
-                        load_filters(chunk + 1)
-                    if chunk + 1 < CHUNKS - 1:
-                        open_chunk(chunk + 1, bias_pool, out_pool)
 
         stack.enter_context(tc.manual_schedule())
         with tc.tile_pool(name="early", bufs=1) as early:
             x_sb = early.tile([P, C_IN, SIDE_IN * SIDE_IN], BF16, name="x_sb")
-            padded = [early.tile([P, C_IN, TAPS, ROW], BF16, name="padded%d" % b) for b in range(2)]
 
             def pad_row(h):
                 tile = padded[h % 2]
                 if h == 0:
-                    nc.vector.tensor_copy(
-                        out=tile[:, :, 1:TAPS, 1:ROW],
-                        in_=x_sb[:, :, 0 : SIDE_IN * (TAPS - 1)].rearrange("p c (i w) -> p c i w", w=SIDE_IN),
-                    )
+                    for channels in X_HALVES:
+                        nc.vector.tensor_copy(
+                            out=tile[:, channels, 1:TAPS, 1:ROW],
+                            in_=x_sb[:, channels, 0 : SIDE_IN * (TAPS - 1)].rearrange("p c (i w) -> p c i w", w=SIDE_IN),
+                        )
                     return
                 nc.scalar.copy(
                     out=tile[:].bitcast(F32)[:, :, 0 : TAPS - 1, :],
@@ -276,28 +283,30 @@ def tile_localconv2dlayer_e_kernel(tc, x, filters_words, filters_scales, bias, o
                     banks.append(planes)
                 return banks
 
-            nc.sync.dma_start(out=x_sb[:], in_=x.rearrange("n c h w -> n c (h w)"))
-            nc.vector.memset(raw_scales[:], 0)
+            for channels in X_HALVES:
+                nc.sync.dma_start(out=x_sb[:, channels, :], in_=x[:, channels, :, :].rearrange("n c h w -> n c (h w)"))
+            for chunk in range(CHUNKS):
+                nc.gpsimd.memset(codes[:, SIDE_OUT - 2 + chunk // PASSES, chunk % PASSES, :].bitcast(F32), 0.0)
             for b in range(2):
                 nc.vector.memset(padded[b][:].bitcast(I32), 0)
             nc.vector.memset(zeros[:].bitcast(I32), 0)
             make_identity(nc, identity[:])
-            load_filters(0)
-            open_chunk(0, bias_pool, out_pool)
+            for chunk in range(CHUNKS):
+                load_filters(chunk)
+                if chunk < CHUNKS - 1:
+                    open_chunk(chunk, bias_pool, out_pool)
 
             pad_row(0)
             pad_row(1)
             copy_out(0, transpose_row(0))
             spread_scales(0)
-            load_filters(1)
-            open_chunk(1, bias_pool, out_pool)
             run_step(-1, transpose_row, pad_row)
             regroup_filters(0)
-            for step_no in range(SIDE_OUT - 2):
+            for step_no in range(X_STEPS):
                 run_step(step_no, transpose_row, pad_row)
 
         with tc.tile_pool(name="late", bufs=1, reuse_waits="tile") as late:
             open_chunk(CHUNKS - 1, late, late)
-            for step_no in range(SIDE_OUT - 2, len(steps)):
-                run_step(step_no, None, None)
+            for step_no in range(X_STEPS, len(steps)):
+                run_step(step_no, transpose_row, pad_row)
             add_bias(len(units) - 1)

from contextlib import ExitStack

import concourse.mybir as mybir
from concourse.masks import make_identity

BF16 = mybir.dt.bfloat16
F32 = mybir.dt.float32
I32 = mybir.dt.int32
U32 = mybir.dt.uint32
U8 = mybir.dt.uint8
FP8X4 = mybir.dt.float8_e4m3fn_x4

P = 128
IMAGES = 128
C_IN = 64
SIDE_IN = 9
SIDE_OUT = 8
TAPS = 4
C_OUT = 128
PIXELS = SIDE_OUT * SIDE_OUT
PASSES = 2
ROW = SIDE_IN + 1
ROW_WORDS = ROW // 2
BANK_PLANES = 4
ROW_BANKS = 3
O_CHUNK = 32
CHUNKS = C_OUT // O_CHUNK
CHUNK_GROUPS = PASSES * O_CHUNK
PX_GROUP = 4
GROUPS_ROW = SIDE_OUT // PX_GROUP
N_MOVING = O_CHUNK * PX_GROUP
BANK = 512
LAG = 2
CATCH_UP = 2
ROW_TILES = PASSES * TAPS // 2
X_STEPS = SIDE_OUT - 4

X_HALVES = (slice(0, C_IN // PASSES), slice(C_IN // PASSES, C_IN))

FLOPS = 2 * IMAGES * C_IN * TAPS * TAPS * C_OUT * PIXELS


def tile_localconv2dlayer_e_kernel(tc, x, filters_words, filters_scales, bias, out):
    nc = tc.nc
    with ExitStack() as stack:
        keep = stack.enter_context(tc.tile_pool(name="keep", bufs=1))
        raw_pool = stack.enter_context(tc.tile_pool(name="raw_filters", bufs=CHUNKS))
        moving_pool = stack.enter_context(tc.tile_pool(name="moving", bufs=2))
        bias_pool = stack.enter_context(tc.tile_pool(name="bias", bufs=3))
        out_pool = stack.enter_context(tc.tile_pool(name="result", bufs=3))
        grouped_pool = stack.enter_context(tc.tile_pool(name="grouped", bufs=3))
        bank_pool = stack.enter_context(tc.psum_pool(name="transposed", bufs=4))
        acc_pool = stack.enter_context(tc.psum_pool(name="sums", bufs=2))

        identity = keep.tile([P, P], F32, name="identity")
        zeros = keep.tile([P, 2 * P], BF16, name="zeros")
        rows = [keep.tile([P, IMAGES, 2 * ROW_BANKS * BANK_PLANES], BF16, name="row%d" % b) for b in range(2)]
        padded = [keep.tile([P, C_IN, TAPS, ROW], BF16, name="padded%d" % b) for b in range(2)]
        codes = keep.tile([P, SIDE_OUT, PASSES, SIDE_OUT * IMAGES], U32, name="codes", align_bytes=64)
        code_scales = keep.tile([P, SIDE_OUT, TAPS * IMAGES], U8, name="code_scales", align_bytes=64)
        filter_scales = keep.tile(
            [P, CHUNKS, SIDE_OUT * GROUPS_ROW, PASSES, N_MOVING], U8, name="filter_scales", align_bytes=64
        )

        raws = {}

        def raw_scales(chunk, partitions):
            return (
                codes[partitions, SIDE_OUT - 2 + chunk // PASSES, chunk % PASSES, :]
                .bitcast(I32)
                .rearrange("p (g w) -> p g w", w=PIXELS // 4)
            )

        def load_filters(chunk):
            groups = slice(CHUNK_GROUPS * chunk, CHUNK_GROUPS * (chunk + 1))
            for quadrant in range(4):
                nc.sync.dma_start(
                    out=raw_scales(chunk, slice(32 * quadrant, 32 * quadrant + 4)),
                    in_=filters_scales[groups, 4 * quadrant : 4 * quadrant + 4, :]
                    .rearrange("g r n -> r g n")
                    .bitcast(I32),
                )
            raw = raw_pool.tile([P, CHUNK_GROUPS, PIXELS], I32, name="raw")
            nc.sync.dma_start(
                out=raw[:], in_=filters_words[groups].rearrange("g p n t -> p g (n t)").bitcast(I32)
            )
            raws[chunk] = raw

        def spread_scales(chunk):
            nc.vector.tensor_copy(
                out=filter_scales[:, chunk].bitcast(I32),
                in_=raw_scales(chunk, slice(0, P)).rearrange("p (o f) g -> p g f o", f=PASSES),
            )

        def fill_tile(h, i):
            f, e = divmod(i, TAPS // 2)
            values = rows[h % 2]
            first = ROW * f + 2 * e
            grouped = grouped_pool.tile([P, 2, 2, IMAGES, TAPS], BF16, name="grouped", align_bytes=64)
            nc.scalar.copy(
                out=grouped[:].bitcast(F32)[:, 0, :, :, :],
                in_=values[:].bitcast(F32)[:, :, first // 2 : first // 2 + TAPS].rearrange("p n (b u) -> p b n u", u=2),
            )
            odd_copy = nc.scalar.copy if i == ROW_TILES - 1 else nc.vector.tensor_copy
            odd_copy(
                out=grouped[:, 1, :, :, :],
                in_=values[:, :, first + 1 : first + 1 + 2 * TAPS].rearrange("p n (b j) -> p b n j", j=TAPS),
            )
            return (f, e, grouped)

        def quantise(h, item):
            f, e, grouped = item
            columns = slice(TAPS * IMAGES * e, TAPS * IMAGES * (e + 1))
            nc.vector.quantize_mx(
                out=codes[:, h, f, columns].bitcast(FP8X4),
                scales=code_scales[4 * (2 * f + e) : P, h, :],
                in_=grouped[:].rearrange("p s b n j -> p (s b n j)"),
            )

        biases = {}
        results = {}
        first_step = [LAG * chunk for chunk in range(CHUNKS)]
        first_step[CHUNKS - 1] -= 1
        steps = []
        done = [0] * CHUNKS
        for step_no in range(first_step[CHUNKS - 1] + SIDE_OUT // CATCH_UP):
            jobs = []
            for chunk in range(CHUNKS):
                if step_no >= first_step[chunk]:
                    upto = min(done[chunk] + CATCH_UP, step_no + 1, SIDE_OUT)
                    jobs.extend((chunk, h) for h in range(done[chunk], upto))
                    done[chunk] = upto
            steps.append(jobs)
        units = [unit for jobs in steps for unit in jobs]
        movings = {}
        sums_of = {}

        def open_chunk(chunk, bias_from, result_from):
            bias_sb = bias_from.tile([P, O_CHUNK, PIXELS], BF16, name="bias_sb")
            nc.sync.dma_start(
                out=bias_sb[:].rearrange("p o n -> p (o n)"),
                in_=bias[O_CHUNK * chunk : O_CHUNK * (chunk + 1), :].rearrange("o n -> (o n)").partition_broadcast(P),
            )
            biases[chunk] = bias_sb
            result = result_from.tile([P, O_CHUNK, PIXELS], F32, name="result")
            results[chunk] = result

        def regroup_filters(k):
            chunk, h = units[k]
            moving = moving_pool.tile([P, GROUPS_ROW, PASSES, N_MOVING], I32, name="moving", align_bytes=64)
            nc.vector.tensor_copy(
                out=moving[:].rearrange("p g f (o q) -> p g f o q", q=PX_GROUP),
                in_=raws[chunk][:]
                .rearrange("p (o f) n -> p o f n", f=PASSES)[:, :, :, SIDE_OUT * h : SIDE_OUT * (h + 1)]
                .rearrange("p o f (g q) -> p g f o q", q=PX_GROUP),
            )
            movings[k] = moving

        def multiply(k):
            chunk, h = units[k]
            moving = movings[k]
            sums = acc_pool.tile([P, GROUPS_ROW * BANK], F32, name="sums")
            for g in range(GROUPS_ROW):
                for q in range(PX_GROUP):
                    block = IMAGES * (2 * q + g)
                    in_call = IMAGES * (2 * (q % 2) + g)
                    for f in range(PASSES):
                        nc.tensor.matmul_mx(
                            out=sums[:, BANK * g + N_MOVING * q : BANK * g + N_MOVING * (q + 1)],
                            lhsT=codes[:, h, f, block : block + IMAGES].bitcast(FP8X4),
                            lhsT_scale=code_scales[4 * (2 * f + q // 2) : P, h, in_call : in_call + IMAGES],
                            rhs=moving[:, g, f, :].bitcast(FP8X4),
                            rhs_scale=filter_scales[:, chunk, GROUPS_ROW * h + g, f, :],
                            start=(f == 0),
                            stop=(f == PASSES - 1),
                        )
            sums_of[k] = sums

        def add_bias(k):
            chunk, h = units[k]
            sums = sums_of[k]
            step = N_MOVING + 1
            for g in range(GROUPS_ROW):
                if g == 0:
                    own = sums[:, 0 : PX_GROUP * step].rearrange("p (q r) -> p q r", r=step)[
                        :, :, 0 : N_MOVING - 3 : PX_GROUP
                    ]
                else:
                    own = sums[:, 2 * BANK - PX_GROUP * step : 2 * BANK].rearrange("p (q r) -> p q r", r=step)[
                        :, :, PX_GROUP:step:PX_GROUP
                    ]
                pixels = slice(SIDE_OUT * h + PX_GROUP * g, SIDE_OUT * h + PX_GROUP * (g + 1))
                nc.vector.tensor_tensor(
                    out=results[chunk][:, :, pixels],
                    in0=own.rearrange("p q o -> p o q"),
                    in1=biases[chunk][:, :, pixels],
                    op=mybir.AluOpType.add,
                )
            if h == SIDE_OUT - 1:
                nc.scalar.dma_start(
                    out=out[:, O_CHUNK * chunk : O_CHUNK * (chunk + 1), :, :].rearrange("n o h w -> n o (h w)"),
                    in_=results[chunk][:],
                )

        def copy_out(h, banks):
            words = rows[h % 2][:].bitcast(F32)
            for bank in range(ROW_BANKS):
                nc.scalar.copy(
                    out=words[:, :, BANK_PLANES * bank : BANK_PLANES * (bank + 1)],
                    in_=banks[bank][:].rearrange("p a n -> p n a"),
                )

        def run_step(step_no, transpose_row, pad_row):
            jobs = steps[step_no] if step_no >= 0 else []
            first_unit = sum(len(earlier) for earlier in steps[: max(step_no, 0)])
            row = step_no + 1
            previous = None
            banks = None
            for i in range(max(ROW_TILES, len(jobs))):
                if row < SIDE_OUT and i < ROW_TILES:
                    filled = fill_tile(row, i)
                    if previous is not None:
                        quantise(row, previous)
                    previous = filled
                if i < len(jobs):
                    k = first_unit + i
                    multiply(k)
                    if k + 1 < len(units):
                        regroup_filters(k + 1)
                    if k >= 1:
                        add_bias(k - 1)
                if i == 0 and row + 1 < SIDE_OUT:
                    banks = transpose_row(row + 1)
            if previous is not None:
                quantise(row, previous)
            if banks is not None:
                copy_out(row + 1, banks)
            if row + 2 < SIDE_OUT:
                pad_row(row + 2)
            for chunk in range(1, CHUNKS):
                if first_step[chunk] == row:
                    spread_scales(chunk)

        stack.enter_context(tc.manual_schedule())
        with tc.tile_pool(name="early", bufs=1) as early:
            x_sb = early.tile([P, C_IN, SIDE_IN * SIDE_IN], BF16, name="x_sb")

            def pad_row(h):
                tile = padded[h % 2]
                if h == 0:
                    for channels in X_HALVES:
                        nc.vector.tensor_copy(
                            out=tile[:, channels, 1:TAPS, 1:ROW],
                            in_=x_sb[:, channels, 0 : SIDE_IN * (TAPS - 1)].rearrange("p c (i w) -> p c i w", w=SIDE_IN),
                        )
                    return
                nc.scalar.copy(
                    out=tile[:].bitcast(F32)[:, :, 0 : TAPS - 1, :],
                    in_=padded[(h - 1) % 2][:].bitcast(F32)[:, :, 1:TAPS, :],
                )
                bottom = h + TAPS - 2
                if bottom < SIDE_IN:
                    nc.scalar.copy(
                        out=tile[:, :, TAPS - 1, 1:ROW], in_=x_sb[:, :, SIDE_IN * bottom : SIDE_IN * (bottom + 1)]
                    )
                else:
                    nc.scalar.copy(
                        out=tile[:, :, TAPS - 1, 1:ROW],
                        in_=zeros[:, 0:SIDE_IN].unsqueeze(1).to_broadcast([P, C_IN, SIDE_IN]),
                    )

            def transpose_row(h):
                source = padded[h % 2][:].bitcast(F32).rearrange("p c i a -> p (c i) a")
                banks = []
                for bank in range(ROW_BANKS):
                    planes = bank_pool.tile([P, BANK_PLANES, IMAGES], F32, name="planes")
                    for m in range(BANK_PLANES):
                        f, a = divmod(BANK_PLANES * bank + m, ROW_WORDS)
                        if f < PASSES:
                            nc.tensor.transpose(planes[:, m, :], source[:, P * f : P * (f + 1), a], identity[:])
                        else:
                            nc.tensor.transpose(planes[:, m, :], zeros[:].bitcast(F32), identity[:])
                    banks.append(planes)
                return banks

            for channels in X_HALVES:
                nc.sync.dma_start(out=x_sb[:, channels, :], in_=x[:, channels, :, :].rearrange("n c h w -> n c (h w)"))
            for chunk in range(CHUNKS):
                nc.gpsimd.memset(codes[:, SIDE_OUT - 2 + chunk // PASSES, chunk % PASSES, :].bitcast(F32), 0.0)
            for b in range(2):
                nc.vector.memset(padded[b][:].bitcast(I32), 0)
            nc.vector.memset(zeros[:].bitcast(I32), 0)
            make_identity(nc, identity[:])
            for chunk in range(CHUNKS):
                load_filters(chunk)
                if chunk < CHUNKS - 1:
                    open_chunk(chunk, bias_pool, out_pool)

            pad_row(0)
            pad_row(1)
            copy_out(0, transpose_row(0))
            spread_scales(0)
            run_step(-1, transpose_row, pad_row)
            regroup_filters(0)
            for step_no in range(X_STEPS):
                run_step(step_no, transpose_row, pad_row)

        with tc.tile_pool(name="late", bufs=1, reuse_waits="tile") as late:
            open_chunk(CHUNKS - 1, late, late)
            for step_no in range(X_STEPS, len(steps)):
                run_step(step_no, transpose_row, pad_row)
            add_bias(len(units) - 1)
